import numpy as np
import ml_dtypes


def mxq(x, axis, fmt="e4m3"):
    dtype, down = {"e4m3": (ml_dtypes.float8_e4m3fn, 7), "e5m2": (ml_dtypes.float8_e5m2, 14)}[fmt]
    v = np.moveaxis(np.asarray(x, np.float32).astype(ml_dtypes.bfloat16).astype(np.float64), axis, -1)
    blocks = v.reshape(v.shape[:-1] + (-1, 32))
    amax = np.abs(blocks).max(-1, keepdims=True)
    byte = np.maximum(np.where(amax > 0, np.frexp(amax)[1] - 1 + 127, 0) - down, 1)
    scale = np.exp2(byte - 127.0)
    codes = (blocks / scale).astype(np.float32).astype(dtype).astype(np.float64)
    return np.moveaxis((codes * scale).reshape(v.shape), -1, axis)


WIDE = False


def mx_kscale(k):
    if not WIDE:
        return np.ones(k)
    levels = np.array([10, -10, 5, -5, 0])
    if k % 512:
        return np.exp2(np.random.permutation(np.resize(levels, k // 32))).repeat(32)
    a = np.empty((k // 512, 16))
    for p in range(k // 512):
        a[p, :8] = np.random.permutation(np.resize(levels, 8))
        for g in range(8):
            far = levels[np.abs(levels - a[p, g]) >= 10]
            a[p, g + 8] = far[np.random.randint(len(far))]
    return np.exp2(a.ravel()).repeat(32)


BF16 = ml_dtypes.bfloat16


def bf(x):
    return np.asarray(x, np.float32).astype(BF16)


def f64(x):
    return np.asarray(x).astype(np.float64)


B, S, IN, OUT = 4, 128, 2048, 2048


def setup_inputs():
    s = mx_kscale(IN)
    w = np.random.standard_normal((OUT, IN + 1))
    w[:, :IN] *= 0.25 / np.sqrt(IN) / s
    w[:, IN] *= 0.5
    return {"x": bf(np.random.standard_normal((B, S, IN)) * s), "weight": bf(w)}


def reference(x, weight):
    w = f64(weight)
    in_features = w.shape[1] - 1
    xf = f64(x).reshape(-1, in_features)
    wm, wb = w[:, :in_features], w[:, in_features]
    xq = mxq(xf, 1, "e4m3")
    wq = mxq(wm, 1, "e4m3")
    lin = (xq @ wq.T) + wb
    ab = (np.abs(xq) @ np.abs(wq).T) + np.abs(wb)
    return 0.5 * (lin + ab)

@@ -1,0 +1,159 @@
+from contextlib import ExitStack
+
+import concourse.mybir as mybir
+from concourse.masks import make_identity
+
+F32 = mybir.dt.float32
+BF16 = mybir.dt.bfloat16
+I32 = mybir.dt.int32
+U8 = mybir.dt.uint8
+FP8X4 = mybir.dt.float8_e4m3fn_x4
+ALU = mybir.AluOpType
+ACT = mybir.ActivationFunctionType
+
+P = 128
+PACK = 4
+K = 2048
+PASSES = K // (P * PACK)
+TOKENS = 512
+OUT = 2048
+BLOCK = 256
+ROW_TILES = BLOCK // P
+X_BLOCKS = TOKENS // BLOCK
+W_BLOCKS = OUT // BLOCK
+ROW_PITCH = K + 32
+AHEAD = 4
+NO_SIGNS = 0x7FFF7FFF
+
+FLOPS = 2 * 2 * TOKENS * K * OUT
+
+
+def tile_skanlinear_kernel(tc, x, weight, out):
+    nc = tc.nc
+    x2 = x.flatten_outer_dims()
+    out_tiles = out.rearrange("(t p) o -> p t o", p=P)
+
+    with ExitStack() as stack:
+        const = stack.enter_context(tc.tile_pool(name="const", bufs=1))
+        raw_pool = stack.enter_context(tc.tile_pool(name="raw", bufs=8))
+        grouped_pool = stack.enter_context(tc.tile_pool(name="grouped", bufs=3))
+        plain_pool = stack.enter_context(tc.tile_pool(name="plain", bufs=2))
+        keep = stack.enter_context(tc.tile_pool(name="keep", bufs=1))
+        y_pool = stack.enter_context(tc.tile_pool(name="y", bufs=4))
+        flip_psum = stack.enter_context(tc.psum_pool(name="flip", bufs=4))
+        acc_psum = stack.enter_context(tc.psum_pool(name="acc", bufs=3))
+        bias_psum = stack.enter_context(tc.psum_pool(name="bias", bufs=1))
+
+        ident_f32 = const.tile([P, P], F32)
+        make_identity(nc, ident_f32[:])
+        ident_bf16 = const.tile([P, P], BF16)
+        make_identity(nc, ident_bf16[:])
+
+        bias_rows = const.tile([P, OUT], F32)
+
+        sources = [("x0", x2[0:BLOCK, :], None), ("w0", weight[0:BLOCK, :], 0), ("x1", x2[BLOCK : 2 * BLOCK, :], None)]
+        for b in range(1, W_BLOCKS):
+            sources.append(("w%d" % b, weight[b * BLOCK : (b + 1) * BLOCK, :], b))
+
+        def load(rows):
+            raw = raw_pool.tile([P, ROW_TILES, ROW_PITCH], BF16)
+            for r in range(ROW_TILES):
+                nc.sync.dma_start(out=raw[:, r, 0 : rows.shape[1]], in_=rows[r * P : (r + 1) * P, :])
+            return raw
+
+        def spread_bias(b, raw):
+            bank = bias_psum.tile([P, BLOCK], F32)
+            for r in range(ROW_TILES):
+                nc.tensor.matmul(
+                    out=bank[:, r * P : (r + 1) * P],
+                    lhsT=raw[:, r, K : K + 1].to_broadcast([P, P]),
+                    rhs=ident_bf16[:],
+                    start=True,
+                    stop=True,
+                )
+            nc.scalar.activation(out=bias_rows[:, b * BLOCK : (b + 1) * BLOCK], in_=bank[:], func=ACT.Relu)
+
+        def transpose(raw):
+            words = raw[:, :, 0:K].bitcast(F32)
+            grouped = grouped_pool.tile([P, PASSES, BLOCK, PACK], BF16, align_bytes=64)
+            grouped_words = grouped[:].bitcast(F32)
+            for g in range(PASSES):
+                bank = flip_psum.tile([P, 2, BLOCK], F32, tag="bank")
+                for u in range(2):
+                    for r in range(ROW_TILES):
+                        nc.tensor.transpose(
+                            bank[:, u, r * P : (r + 1) * P], words[:, r, 2 * g * P + u : 2 * (g + 1) * P : 2], ident_f32[:]
+                        )
+                nc.scalar.copy(out=grouped_words[:, g, :, :], in_=bank[:].rearrange("p u o -> p o u"))
+            return grouped
+
+        def quantise_one(name, values):
+            codes = keep.tile([P, PASSES, BLOCK], I32, name="codes_" + name, align_bytes=64)
+            scales = keep.tile([P, PASSES, BLOCK], U8, name="scales_" + name, align_bytes=64)
+            nc.vector.quantize_mx(
+                out=codes[:].rearrange("p g o -> p (g o)").bitcast(FP8X4),
+                scales=scales[:].rearrange("p g o -> p (g o)"),
+                in_=values[:].rearrange("p g o t -> p (g o t)"),
+            )
+            return (codes, scales)
+
+        def quantise(label, grouped):
+            plain = plain_pool.tile([P, PASSES, BLOCK, PACK], BF16, align_bytes=64)
+            nc.vector.tensor_scalar(
+                out=plain[:].bitcast(I32),
+                in0=grouped[:].bitcast(I32),
+                scalar1=NO_SIGNS,
+                scalar2=None,
+                op0=ALU.bitwise_and,
+            )
+            return (quantise_one(label, grouped), quantise_one("abs_" + label, plain))
+
+        def multiply(b, x_ready, w_ready):
+            cols = slice(b * BLOCK, (b + 1) * BLOCK)
+            for pair in range(X_BLOCKS):
+                acc = acc_psum.tile([P, ROW_TILES, BLOCK], F32)
+                for half in range(ROW_TILES):
+                    tokens = slice(half * P, (half + 1) * P)
+                    for kind in range(2):
+                        x_codes, x_scales = x_ready[pair][kind]
+                        w_codes, w_scales = w_ready[kind]
+                        for g in range(PASSES):
+                            nc.tensor.matmul_mx(
+                                out=acc[:, half, :],
+                                lhsT=x_codes[:, g, tokens].bitcast(FP8X4),
+                                lhsT_scale=x_scales[:, g, tokens],
+                                rhs=w_codes[:, g, :].bitcast(FP8X4),
+                                rhs_scale=w_scales[:, g, :],
+                                start=(kind == 0 and g == 0),
+                                stop=(kind == 1 and g == PASSES - 1),
+                            )
+                y = y_pool.tile([P, ROW_TILES, BLOCK], F32)
+                nc.vector.scalar_tensor_tensor(
+                    out=y[:],
+                    in0=acc[:],
+                    scalar=0.5,
+                    in1=bias_rows[:, cols].unsqueeze(1).to_broadcast([P, ROW_TILES, BLOCK]),
+                    op0=ALU.mult,
+                    op1=ALU.add,
+                )
+                nc.sync.dma_start(
+                    out=out_tiles[:, pair * ROW_TILES : (pair + 1) * ROW_TILES, cols], in_=y[:]
+                )
+
+        raws = []
+        for source in sources:
+            raws.append(load(source[1]))
+
+        grouped_tiles = {}
+        ready = {}
+        for step in range(W_BLOCKS + AHEAD):
+            if step < len(sources):
+                grouped_tiles[step] = transpose(raws[step])
+                if sources[step][2] is not None:
+                    spread_bias(sources[step][2], raws[step])
+            if 1 <= step <= len(sources):
+                label = sources[step - 1][0]
+                ready[label] = quantise(label, grouped_tiles[step - 1])
+            if step >= AHEAD:
+                b = step - AHEAD
+                multiply(b, [ready["x0"], ready["x1"]], ready["w%d" % b])

@@ -23,6 +23,8 @@ X_BLOCKS = TOKENS // BLOCK
 W_BLOCKS = OUT // BLOCK
 ROW_PITCH = K + 32
 AHEAD = 4
+STRIDED = 3
+SORT_AHEAD = 2
 NO_SIGNS = 0x7FFF7FFF
 
 FLOPS = 2 * 2 * TOKENS * K * OUT
@@ -35,10 +37,12 @@ def tile_skanlinear_kernel(tc, x, weight, out):
 
     with ExitStack() as stack:
         const = stack.enter_context(tc.tile_pool(name="const", bufs=1))
-        raw_pool = stack.enter_context(tc.tile_pool(name="raw", bufs=8))
+        raw_pool = stack.enter_context(tc.tile_pool(name="raw", bufs=10))
+        sorted_pool = stack.enter_context(tc.tile_pool(name="sorted", bufs=3))
         grouped_pool = stack.enter_context(tc.tile_pool(name="grouped", bufs=3))
         plain_pool = stack.enter_context(tc.tile_pool(name="plain", bufs=2))
         keep = stack.enter_context(tc.tile_pool(name="keep", bufs=1))
+        w_pool = stack.enter_context(tc.tile_pool(name="w", bufs=4))
         y_pool = stack.enter_context(tc.tile_pool(name="y", bufs=4))
         flip_psum = stack.enter_context(tc.psum_pool(name="flip", bufs=4))
         acc_psum = stack.enter_context(tc.psum_pool(name="acc", bufs=3))
@@ -73,23 +77,33 @@ def tile_skanlinear_kernel(tc, x, weight, out):
                 )
             nc.scalar.activation(out=bias_rows[:, b * BLOCK : (b + 1) * BLOCK], in_=bank[:], func=ACT.Relu)
 
-        def transpose(raw):
-            words = raw[:, :, 0:K].bitcast(F32)
+        def sort_words(raw):
+            done = sorted_pool.tile([P, ROW_TILES, 2, K // 4], F32)
+            for r in range(ROW_TILES):
+                nc.scalar.copy(
+                    out=done[:, r, :, :],
+                    in_=raw[:, r, 0:K].bitcast(F32).rearrange("p (w u) -> p u w", u=2),
+                )
+            return done
+
+        def transpose(words, strided):
             grouped = grouped_pool.tile([P, PASSES, BLOCK, PACK], BF16, align_bytes=64)
             grouped_words = grouped[:].bitcast(F32)
             for g in range(PASSES):
                 bank = flip_psum.tile([P, 2, BLOCK], F32, tag="bank")
                 for u in range(2):
                     for r in range(ROW_TILES):
-                        nc.tensor.transpose(
-                            bank[:, u, r * P : (r + 1) * P], words[:, r, 2 * g * P + u : 2 * (g + 1) * P : 2], ident_f32[:]
-                        )
+                        if strided:
+                            part = words[:, r, 2 * g * P + u : 2 * (g + 1) * P : 2]
+                        else:
+                            part = words[:, r, u, g * P : (g + 1) * P]
+                        nc.tensor.transpose(bank[:, u, r * P : (r + 1) * P], part, ident_f32[:])
                 nc.scalar.copy(out=grouped_words[:, g, :, :], in_=bank[:].rearrange("p u o -> p o u"))
             return grouped
 
-        def quantise_one(name, values):
-            codes = keep.tile([P, PASSES, BLOCK], I32, name="codes_" + name, align_bytes=64)
-            scales = keep.tile([P, PASSES, BLOCK], U8, name="scales_" + name, align_bytes=64)
+        def quantise_one(pool, name, values):
+            codes = pool.tile([P, PASSES, BLOCK], I32, name="codes_" + name, align_bytes=64)
+            scales = pool.tile([P, PASSES, BLOCK], U8, name="scales_" + name, align_bytes=64)
             nc.vector.quantize_mx(
                 out=codes[:].rearrange("p g o -> p (g o)").bitcast(FP8X4),
                 scales=scales[:].rearrange("p g o -> p (g o)"),
@@ -106,7 +120,8 @@ def tile_skanlinear_kernel(tc, x, weight, out):
                 scalar2=None,
                 op0=ALU.bitwise_and,
             )
-            return (quantise_one(label, grouped), quantise_one("abs_" + label, plain))
+            pool, name = (keep, label) if label[0] == "x" else (w_pool, "w")
+            return (quantise_one(pool, name, grouped), quantise_one(pool, "abs_" + name, plain))
 
         def multiply(b, x_ready, w_ready):
             cols = slice(b * BLOCK, (b + 1) * BLOCK)
@@ -144,13 +159,19 @@ def tile_skanlinear_kernel(tc, x, weight, out):
         for source in sources:
             raws.append(load(source[1]))
 
+        sorted_tiles = {}
         grouped_tiles = {}
         ready = {}
         for step in range(W_BLOCKS + AHEAD):
             if step < len(sources):
-                grouped_tiles[step] = transpose(raws[step])
+                if step < STRIDED:
+                    grouped_tiles[step] = transpose(raws[step][:, :, 0:K].bitcast(F32), True)
+                else:
+                    grouped_tiles[step] = transpose(sorted_tiles[step], False)
                 if sources[step][2] is not None:
                     spread_bias(sources[step][2], raws[step])
+            if STRIDED <= step + SORT_AHEAD < len(sources):
+                sorted_tiles[step + SORT_AHEAD] = sort_words(raws[step + SORT_AHEAD])
             if 1 <= step <= len(sources):
                 label = sources[step - 1][0]
                 ready[label] = quantise(label, grouped_tiles[step - 1])

@@ -15,16 +15,17 @@ P = 128
 PACK = 4
 K = 2048
 PASSES = K // (P * PACK)
+HALF = K // 2
 TOKENS = 512
 OUT = 2048
-BLOCK = 256
-ROW_TILES = BLOCK // P
-X_BLOCKS = TOKENS // BLOCK
-W_BLOCKS = OUT // BLOCK
-ROW_PITCH = K + 32
-AHEAD = 4
-STRIDED = 3
-SORT_AHEAD = 2
+ROWS = 512
+ROW_TILES = ROWS // P
+TOKEN_TILES = TOKENS // P
+W_BLOCKS = OUT // ROWS
+PAIR = 256
+ROW_PITCH = HALF + 32
+PASS_WORDS = 256
+FIRST_SORTED = 6
 NO_SIGNS = 0x7FFF7FFF
 
 FLOPS = 2 * 2 * TOKENS * K * OUT
@@ -38,15 +39,14 @@ def tile_skanlinear_kernel(tc, x, weight, out):
     with ExitStack() as stack:
         const = stack.enter_context(tc.tile_pool(name="const", bufs=1))
         raw_pool = stack.enter_context(tc.tile_pool(name="raw", bufs=10))
-        sorted_pool = stack.enter_context(tc.tile_pool(name="sorted", bufs=3))
-        grouped_pool = stack.enter_context(tc.tile_pool(name="grouped", bufs=3))
-        plain_pool = stack.enter_context(tc.tile_pool(name="plain", bufs=2))
-        keep = stack.enter_context(tc.tile_pool(name="keep", bufs=1))
-        w_pool = stack.enter_context(tc.tile_pool(name="w", bufs=4))
+        sorted_pool = stack.enter_context(tc.tile_pool(name="sorted", bufs=6))
+        grouped_pool = stack.enter_context(tc.tile_pool(name="grouped", bufs=5))
+        plain_pool = stack.enter_context(tc.tile_pool(name="plain", bufs=3))
+        x_pool = stack.enter_context(tc.tile_pool(name="x", bufs=1))
+        w_pool = stack.enter_context(tc.tile_pool(name="w", bufs=2))
         y_pool = stack.enter_context(tc.tile_pool(name="y", bufs=4))
         flip_psum = stack.enter_context(tc.psum_pool(name="flip", bufs=4))
-        acc_psum = stack.enter_context(tc.psum_pool(name="acc", bufs=3))
-        bias_psum = stack.enter_context(tc.psum_pool(name="bias", bufs=1))
+        acc_psum = stack.enter_context(tc.psum_pool(name="acc", bufs=4))
 
         ident_f32 = const.tile([P, P], F32)
         make_identity(nc, ident_f32[:])
@@ -55,126 +55,172 @@ def tile_skanlinear_kernel(tc, x, weight, out):
 
         bias_rows = const.tile([P, OUT], F32)
 
-        sources = [("x0", x2[0:BLOCK, :], None), ("w0", weight[0:BLOCK, :], 0), ("x1", x2[BLOCK : 2 * BLOCK, :], None)]
-        for b in range(1, W_BLOCKS):
-            sources.append(("w%d" % b, weight[b * BLOCK : (b + 1) * BLOCK, :], b))
+        raws = {}
 
-        def load(rows):
-            raw = raw_pool.tile([P, ROW_TILES, ROW_PITCH], BF16)
-            for r in range(ROW_TILES):
-                nc.sync.dma_start(out=raw[:, r, 0 : rows.shape[1]], in_=rows[r * P : (r + 1) * P, :])
-            return raw
+        def load(source, h, first, last, per_dma):
+            rows = x2 if source == "x" else weight[source * ROWS : (source + 1) * ROWS, :]
+            view = rows[:, h * HALF + first : h * HALF + last].rearrange("(r p) k -> p r k", p=P)
+            if first == 0:
+                raws[(source, h)] = raw_pool.tile([P, ROW_TILES, ROW_PITCH], BF16, name="raw")
+            raw = raws[(source, h)]
+            for r in range(0, ROW_TILES, per_dma):
+                nc.sync.dma_start(out=raw[:, r : r + per_dma, first:last], in_=view[:, r : r + per_dma, :])
 
-        def spread_bias(b, raw):
-            bank = bias_psum.tile([P, BLOCK], F32)
+        def spread_bias(b):
+            bank = flip_psum.tile([P, ROWS], F32, tag="bank")
             for r in range(ROW_TILES):
                 nc.tensor.matmul(
                     out=bank[:, r * P : (r + 1) * P],
-                    lhsT=raw[:, r, K : K + 1].to_broadcast([P, P]),
+                    lhsT=raws[(b, 1)][:, r, HALF : HALF + 1].to_broadcast([P, P]),
                     rhs=ident_bf16[:],
                     start=True,
                     stop=True,
                 )
-            nc.scalar.activation(out=bias_rows[:, b * BLOCK : (b + 1) * BLOCK], in_=bank[:], func=ACT.Relu)
+            nc.scalar.activation(out=bias_rows[:, b * ROWS : (b + 1) * ROWS], in_=bank[:], func=ACT.Relu)
 
-        def sort_words(raw):
-            done = sorted_pool.tile([P, ROW_TILES, 2, K // 4], F32)
-            for r in range(ROW_TILES):
-                nc.scalar.copy(
-                    out=done[:, r, :, :],
-                    in_=raw[:, r, 0:K].bitcast(F32).rearrange("p (w u) -> p u w", u=2),
-                )
-            return done
+        sorted_words = {}
+        grouped_values = {}
+        ready = {}
 
-        def transpose(words, strided):
-            grouped = grouped_pool.tile([P, PASSES, BLOCK, PACK], BF16, align_bytes=64)
-            grouped_words = grouped[:].bitcast(F32)
-            for g in range(PASSES):
-                bank = flip_psum.tile([P, 2, BLOCK], F32, tag="bank")
+        def pass_words(source, g):
+            first = (g % 2) * PASS_WORDS * 2
+            return raws[(source, g // 2)][:, :, first : first + PASS_WORDS * 2].bitcast(F32)
+
+        def sort_words(source, g):
+            done = sorted_pool.tile([P, ROW_TILES, 2, P], F32)
+            nc.scalar.copy(out=done[:], in_=pass_words(source, g).rearrange("p r (w u) -> p r u w", u=2))
+            sorted_words[(source, g)] = done
+
+        def transpose(source, g):
+            grouped = grouped_pool.tile([P, ROWS, PACK], BF16, align_bytes=64)
+            words = grouped[:].rearrange("p o t -> p (o t)").bitcast(F32).rearrange("p (o u) -> p o u", u=2)
+            for first in range(0, ROWS, PAIR):
+                bank = flip_psum.tile([P, 2, PAIR], F32, tag="bank")
                 for u in range(2):
-                    for r in range(ROW_TILES):
-                        if strided:
-                            part = words[:, r, 2 * g * P + u : 2 * (g + 1) * P : 2]
+                    for r in range(PAIR // P):
+                        tile_number = first // P + r
+                        if (source, g) in sorted_words:
+                            part = sorted_words[(source, g)][:, tile_number, u, :]
                         else:
-                            part = words[:, r, u, g * P : (g + 1) * P]
+                            part = pass_words(source, g)[:, tile_number, u::2]
                         nc.tensor.transpose(bank[:, u, r * P : (r + 1) * P], part, ident_f32[:])
-                nc.scalar.copy(out=grouped_words[:, g, :, :], in_=bank[:].rearrange("p u o -> p o u"))
-            return grouped
+                nc.scalar.copy(out=words[:, first : first + PAIR, :], in_=bank[:].rearrange("p u o -> p o u"))
+            grouped_values[(source, g)] = grouped
 
         def quantise_one(pool, name, values):
-            codes = pool.tile([P, PASSES, BLOCK], I32, name="codes_" + name, align_bytes=64)
-            scales = pool.tile([P, PASSES, BLOCK], U8, name="scales_" + name, align_bytes=64)
+            codes = pool.tile([P, ROWS], I32, name="codes_" + name, align_bytes=64)
+            scales = pool.tile([P, ROWS], U8, name="scales_" + name, align_bytes=64)
             nc.vector.quantize_mx(
-                out=codes[:].rearrange("p g o -> p (g o)").bitcast(FP8X4),
-                scales=scales[:].rearrange("p g o -> p (g o)"),
-                in_=values[:].rearrange("p g o t -> p (g o t)"),
+                out=codes[:].bitcast(FP8X4), scales=scales[:], in_=values[:].rearrange("p o t -> p (o t)")
             )
             return (codes, scales)
 
-        def quantise(label, grouped):
-            plain = plain_pool.tile([P, PASSES, BLOCK, PACK], BF16, align_bytes=64)
+        plain_values = {}
+
+        def quantise_signed(source, g):
+            pool, name = (x_pool, "x%d" % g) if source == "x" else (w_pool, "w%d" % g)
+            ready[(source, g, 0)] = quantise_one(pool, name, grouped_values[(source, g)])
+
+        def clear_signs(source, g):
+            plain = plain_pool.tile([P, ROWS, PACK], BF16, align_bytes=64)
             nc.vector.tensor_scalar(
                 out=plain[:].bitcast(I32),
-                in0=grouped[:].bitcast(I32),
+                in0=grouped_values[(source, g)][:].bitcast(I32),
                 scalar1=NO_SIGNS,
                 scalar2=None,
                 op0=ALU.bitwise_and,
             )
-            pool, name = (keep, label) if label[0] == "x" else (w_pool, "w")
-            return (quantise_one(pool, name, grouped), quantise_one(pool, "abs_" + name, plain))
+            plain_values[(source, g)] = plain
 
-        def multiply(b, x_ready, w_ready):
-            cols = slice(b * BLOCK, (b + 1) * BLOCK)
-            for pair in range(X_BLOCKS):
-                acc = acc_psum.tile([P, ROW_TILES, BLOCK], F32)
-                for half in range(ROW_TILES):
-                    tokens = slice(half * P, (half + 1) * P)
+        def quantise_plain(source, g):
+            pool, name = (x_pool, "abs_x%d" % g) if source == "x" else (w_pool, "abs_w%d" % g)
+            ready[(source, g, 1)] = quantise_one(pool, name, plain_values[(source, g)])
+
+        acc = {}
+
+        def multiply(b, t, g, kind):
+            tokens = slice(t * P, (t + 1) * P)
+            if g == 0 and kind == 0:
+                acc[t] = acc_psum.tile([P, ROWS], F32, name="acc")
+            x_codes, x_scales = ready[("x", g, kind)]
+            w_codes, w_scales = ready[(b, g, kind)]
+            nc.tensor.matmul_mx(
+                out=acc[t][:],
+                lhsT=x_codes[:, tokens].bitcast(FP8X4),
+                lhsT_scale=x_scales[:, tokens],
+                rhs=w_codes[:].bitcast(FP8X4),
+                rhs_scale=w_scales[:],
+                start=(g == 0 and kind == 0),
+                stop=(g == PASSES - 1 and kind == 1),
+            )
+
+        def finish(b, t):
+            cols = slice(b * ROWS, (b + 1) * ROWS)
+            y = y_pool.tile([P, ROWS], F32)
+            nc.vector.scalar_tensor_tensor(
+                out=y[:], in0=acc[t][:], scalar=0.5, in1=bias_rows[:, cols], op0=ALU.mult, op1=ALU.add
+            )
+            nc.sync.dma_start(out=out_tiles[:, t, cols], in_=y[:])
+
+        stack.enter_context(tc.manual_schedule())
+
+        load("x", 0, 0, HALF // 2, 1)
+        load(0, 0, 0, HALF // 2, 2)
+        load("x", 0, HALF // 2, HALF, 2)
+        load(0, 0, HALF // 2, HALF, 2)
+        load("x", 1, 0, HALF, 2)
+        load(0, 1, 0, HALF + 1, 2)
+        for b in range(1, W_BLOCKS):
+            load(b, 0, 0, HALF, ROW_TILES)
+            load(b, 1, 0, HALF + 1, ROW_TILES)
+
+        head = []
+        for g in range(PASSES):
+            head += [("x", g), (0, g)]
+        head += [(1, 0), (1, 1), (1, 2), (1, 3)]
+        for i in range(9):
+            transpose(*head[i])
+            quantise_signed(*head[i])
+            if i > 0:
+                quantise_plain(*head[i - 1])
+            clear_signs(*head[i])
+            if i + 2 >= FIRST_SORTED:
+                sort_words(*head[i + 2])
+            if 2 <= i < 8:
+                for t in range(TOKEN_TILES):
+                    multiply(0, t, (i - 2) // 2, i % 2)
+        spread_bias(0)
+        transpose(1, 1)
+        sort_words(1, 3)
+        rest = [lambda: quantise_signed(1, 1), lambda: quantise_plain(1, 0), lambda: clear_signs(1, 1), lambda: quantise_plain(1, 1)]
+        for t in range(TOKEN_TILES):
+            multiply(0, t, PASSES - 1, 0)
+            multiply(0, t, PASSES - 1, 1)
+            finish(0, t)
+            rest[t]()
+
+        pairs = [(b, g) for b in range(1, W_BLOCKS) for g in (0, 2)]
+        for i in range(len(pairs)):
+            b, g = pairs[i]
+            vector_work = []
+            if i + 1 < len(pairs):
+                nb, ng = pairs[i + 1]
+                transpose(nb, ng)
+                transpose(nb, ng + 1)
+                if ng == 2:
+                    spread_bias(nb)
+                vector_work = [(quantise_signed, ng), (clear_signs, ng), (quantise_signed, ng + 1), (quantise_plain, ng), (clear_signs, ng + 1), (quantise_plain, ng + 1)]
+            if i + 2 < len(pairs):
+                sort_words(pairs[i + 2][0], pairs[i + 2][1])
+                sort_words(pairs[i + 2][0], pairs[i + 2][1] + 1)
+            for t in range(TOKEN_TILES):
+                for pass_number in (g, g + 1):
                     for kind in range(2):
-                        x_codes, x_scales = x_ready[pair][kind]
-                        w_codes, w_scales = w_ready[kind]
-                        for g in range(PASSES):
-                            nc.tensor.matmul_mx(
-                                out=acc[:, half, :],
-                                lhsT=x_codes[:, g, tokens].bitcast(FP8X4),
-                                lhsT_scale=x_scales[:, g, tokens],
-                                rhs=w_codes[:, g, :].bitcast(FP8X4),
-                                rhs_scale=w_scales[:, g, :],
-                                start=(kind == 0 and g == 0),
-                                stop=(kind == 1 and g == PASSES - 1),
-                            )
-                y = y_pool.tile([P, ROW_TILES, BLOCK], F32)
-                nc.vector.scalar_tensor_tensor(
-                    out=y[:],
-                    in0=acc[:],
-                    scalar=0.5,
-                    in1=bias_rows[:, cols].unsqueeze(1).to_broadcast([P, ROW_TILES, BLOCK]),
-                    op0=ALU.mult,
-                    op1=ALU.add,
-                )
-                nc.sync.dma_start(
-                    out=out_tiles[:, pair * ROW_TILES : (pair + 1) * ROW_TILES, cols], in_=y[:]
-                )
-
-        raws = []
-        for source in sources:
-            raws.append(load(source[1]))
-
-        sorted_tiles = {}
-        grouped_tiles = {}
-        ready = {}
-        for step in range(W_BLOCKS + AHEAD):
-            if step < len(sources):
-                if step < STRIDED:
-                    grouped_tiles[step] = transpose(raws[step][:, :, 0:K].bitcast(F32), True)
-                else:
-                    grouped_tiles[step] = transpose(sorted_tiles[step], False)
-                if sources[step][2] is not None:
-                    spread_bias(sources[step][2], raws[step])
-            if STRIDED <= step + SORT_AHEAD < len(sources):
-                sorted_tiles[step + SORT_AHEAD] = sort_words(raws[step + SORT_AHEAD])
-            if 1 <= step <= len(sources):
-                label = sources[step - 1][0]
-                ready[label] = quantise(label, grouped_tiles[step - 1])
-            if step >= AHEAD:
-                b = step - AHEAD
-                multiply(b, [ready["x0"], ready["x1"]], ready["w%d" % b])
+                        multiply(b, t, pass_number, kind)
+                for step in range(2 if t > 0 else 1):
+                    if len(vector_work) > 0:
+                        work = vector_work[0]
+                        vector_work = vector_work[1:]
+                        work[0](nb, work[1])
+                if g == 2:
+                    finish(b, t)

@@ -25,7 +25,7 @@ W_BLOCKS = OUT // ROWS
 PAIR = 256
 ROW_PITCH = HALF + 32
 PASS_WORDS = 256
-FIRST_SORTED = 6
+FIRST_SORTED = 3
 NO_SIGNS = 0x7FFF7FFF
 
 FLOPS = 2 * 2 * TOKENS * K * OUT
@@ -138,89 +138,87 @@ def tile_skanlinear_kernel(tc, x, weight, out):
 
         acc = {}
 
-        def multiply(b, t, g, kind):
+        def multiply(b, t, g, kind, cols=slice(0, ROWS)):
             tokens = slice(t * P, (t + 1) * P)
             if g == 0 and kind == 0:
-                acc[t] = acc_psum.tile([P, ROWS], F32, name="acc")
+                acc[t] = acc_psum.tile([P, cols.stop - cols.start], F32, name="acc")
             x_codes, x_scales = ready[("x", g, kind)]
             w_codes, w_scales = ready[(b, g, kind)]
             nc.tensor.matmul_mx(
                 out=acc[t][:],
                 lhsT=x_codes[:, tokens].bitcast(FP8X4),
                 lhsT_scale=x_scales[:, tokens],
-                rhs=w_codes[:].bitcast(FP8X4),
-                rhs_scale=w_scales[:],
+                rhs=w_codes[:, cols].bitcast(FP8X4),
+                rhs_scale=w_scales[:, cols],
                 start=(g == 0 and kind == 0),
                 stop=(g == PASSES - 1 and kind == 1),
             )
 
-        def finish(b, t):
-            cols = slice(b * ROWS, (b + 1) * ROWS)
-            y = y_pool.tile([P, ROWS], F32)
+        def finish(b, t, cols=slice(0, ROWS)):
+            out_cols = slice(b * ROWS + cols.start, b * ROWS + cols.stop)
+            y = y_pool.tile([P, cols.stop - cols.start], F32)
             nc.vector.scalar_tensor_tensor(
-                out=y[:], in0=acc[t][:], scalar=0.5, in1=bias_rows[:, cols], op0=ALU.mult, op1=ALU.add
+                out=y[:], in0=acc[t][:], scalar=0.5, in1=bias_rows[:, out_cols], op0=ALU.mult, op1=ALU.add
             )
-            nc.sync.dma_start(out=out_tiles[:, t, cols], in_=y[:])
+            nc.sync.dma_start(out=out_tiles[:, t, out_cols], in_=y[:])
 
         stack.enter_context(tc.manual_schedule())
 
         load("x", 0, 0, HALF // 2, 1)
-        load(0, 0, 0, HALF // 2, 2)
-        load("x", 0, HALF // 2, HALF, 2)
-        load(0, 0, HALF // 2, HALF, 2)
+        load(0, 0, 0, HALF // 2, 1)
+        load("x", 0, HALF // 2, HALF, 1)
+        load(0, 0, HALF // 2, HALF, 1)
         load("x", 1, 0, HALF, 2)
         load(0, 1, 0, HALF + 1, 2)
         for b in range(1, W_BLOCKS):
             load(b, 0, 0, HALF, ROW_TILES)
             load(b, 1, 0, HALF + 1, ROW_TILES)
 
-        head = []
-        for g in range(PASSES):
-            head += [("x", g), (0, g)]
-        head += [(1, 0), (1, 1), (1, 2), (1, 3)]
-        for i in range(9):
-            transpose(*head[i])
-            quantise_signed(*head[i])
-            if i > 0:
-                quantise_plain(*head[i - 1])
-            clear_signs(*head[i])
-            if i + 2 >= FIRST_SORTED:
-                sort_words(*head[i + 2])
-            if 2 <= i < 8:
-                for t in range(TOKEN_TILES):
-                    multiply(0, t, (i - 2) // 2, i % 2)
-        spread_bias(0)
-        transpose(1, 1)
-        sort_words(1, 3)
-        rest = [lambda: quantise_signed(1, 1), lambda: quantise_plain(1, 0), lambda: clear_signs(1, 1), lambda: quantise_plain(1, 1)]
-        for t in range(TOKEN_TILES):
-            multiply(0, t, PASSES - 1, 0)
-            multiply(0, t, PASSES - 1, 1)
-            finish(0, t)
-            rest[t]()
+        pairs = [(("x", g), (0, g)) for g in range(PASSES)]
+        for b in range(1, W_BLOCKS):
+            pairs += [((b, g), (b, g + 1)) for g in range(0, PASSES, 2)]
 
-        pairs = [(b, g) for b in range(1, W_BLOCKS) for g in (0, 2)]
-        for i in range(len(pairs)):
-            b, g = pairs[i]
-            vector_work = []
-            if i + 1 < len(pairs):
-                nb, ng = pairs[i + 1]
-                transpose(nb, ng)
-                transpose(nb, ng + 1)
-                if ng == 2:
-                    spread_bias(nb)
-                vector_work = [(quantise_signed, ng), (clear_signs, ng), (quantise_signed, ng + 1), (quantise_plain, ng), (clear_signs, ng + 1), (quantise_plain, ng + 1)]
-            if i + 2 < len(pairs):
-                sort_words(pairs[i + 2][0], pairs[i + 2][1])
-                sort_words(pairs[i + 2][0], pairs[i + 2][1] + 1)
-            for t in range(TOKEN_TILES):
-                for pass_number in (g, g + 1):
-                    for kind in range(2):
-                        multiply(b, t, pass_number, kind)
-                for step in range(2 if t > 0 else 1):
-                    if len(vector_work) > 0:
-                        work = vector_work[0]
-                        vector_work = vector_work[1:]
-                        work[0](nb, work[1])
-                if g == 2:
-                    finish(b, t)
+        def vector_steps(i):
+            if i == len(pairs):
+                return []
+            if i == 0:
+                order = [(quantise_signed, 0), (clear_signs, 0), (quantise_signed, 1), (quantise_plain, 0), (clear_signs, 1), (quantise_plain, 1)]
+            else:
+                order = [(clear_signs, 0), (quantise_signed, 0), (quantise_plain, 0), (clear_signs, 1), (quantise_signed, 1), (quantise_plain, 1)]
+            return [(call, pairs[i][which]) for call, which in order]
+
+        for i in range(len(pairs) + 1):
+            if i < len(pairs):
+                for unit in pairs[i]:
+                    transpose(*unit)
+                if pairs[i][1][1] == PASSES - 1:
+                    spread_bias(pairs[i][1][0])
+            if FIRST_SORTED <= i + 1 < len(pairs):
+                for unit in pairs[i + 1]:
+                    sort_words(*unit)
+            steps = vector_steps(i)
+            if i > 0:
+                b, last = pairs[i - 1][1]
+                now = [last] if i <= PASSES else [last - 1, last]
+            if i < PASSES:
+                for call, unit in steps:
+                    call(*unit)
+                for kind in range(2 if i > 0 else 0):
+                    for t in range(TOKEN_TILES):
+                        multiply(b, t, last, kind)
+            else:
+                for t in range(TOKEN_TILES):
+                    if b == W_BLOCKS - 1 and t == TOKEN_TILES - 1:
+                        for cols in (slice(0, PAIR), slice(PAIR, ROWS)) if last == PASSES - 1 else ():
+                            for g in range(PASSES):
+                                for kind in range(2):
+                                    multiply(b, t, g, kind, cols)
+                            finish(b, t, cols)
+                        continue
+                    for g in now:
+                        for kind in range(2):
+                            multiply(b, t, g, kind)
+                    for call, unit in steps[2 * t : 2 * t + 2]:
+                        call(*unit)
+                    if last == PASSES - 1:
+                        finish(b, t)

@@ -25,7 +25,6 @@ W_BLOCKS = OUT // ROWS
 PAIR = 256
 ROW_PITCH = HALF + 32
 PASS_WORDS = 256
-FIRST_SORTED = 3
 NO_SIGNS = 0x7FFF7FFF
 
 FLOPS = 2 * 2 * TOKENS * K * OUT
@@ -40,7 +39,7 @@ def tile_skanlinear_kernel(tc, x, weight, out):
         const = stack.enter_context(tc.tile_pool(name="const", bufs=1))
         raw_pool = stack.enter_context(tc.tile_pool(name="raw", bufs=10))
         sorted_pool = stack.enter_context(tc.tile_pool(name="sorted", bufs=6))
-        grouped_pool = stack.enter_context(tc.tile_pool(name="grouped", bufs=5))
+        grouped_pool = stack.enter_context(tc.tile_pool(name="grouped", bufs=7))
         plain_pool = stack.enter_context(tc.tile_pool(name="plain", bufs=3))
         x_pool = stack.enter_context(tc.tile_pool(name="x", bufs=1))
         w_pool = stack.enter_context(tc.tile_pool(name="w", bufs=2))
@@ -164,61 +163,77 @@ def tile_skanlinear_kernel(tc, x, weight, out):
 
         stack.enter_context(tc.manual_schedule())
 
-        load("x", 0, 0, HALF // 2, 1)
-        load(0, 0, 0, HALF // 2, 1)
-        load("x", 0, HALF // 2, HALF, 1)
-        load(0, 0, HALF // 2, HALF, 1)
-        load("x", 1, 0, HALF, 2)
+        for g in range(PASSES):
+            first = (g % 2) * (HALF // 2)
+            load("x", g // 2, first, first + HALF // 2, 1)
+            if g < 2:
+                load(0, 0, first, first + HALF // 2, 1)
         load(0, 1, 0, HALF + 1, 2)
         for b in range(1, W_BLOCKS):
             load(b, 0, 0, HALF, ROW_TILES)
             load(b, 1, 0, HALF + 1, ROW_TILES)
 
-        pairs = [(("x", g), (0, g)) for g in range(PASSES)]
-        for b in range(1, W_BLOCKS):
-            pairs += [((b, g), (b, g + 1)) for g in range(0, PASSES, 2)]
+        def prepare(*units):
+            for unit in units:
+                transpose(*unit)
+            for unit in units:
+                clear_signs(*unit)
+                quantise_signed(*unit)
+                quantise_plain(*unit)
 
-        def vector_steps(i):
-            if i == len(pairs):
-                return []
-            if i == 0:
-                order = [(quantise_signed, 0), (clear_signs, 0), (quantise_signed, 1), (quantise_plain, 0), (clear_signs, 1), (quantise_plain, 1)]
-            else:
-                order = [(clear_signs, 0), (quantise_signed, 0), (quantise_plain, 0), (clear_signs, 1), (quantise_signed, 1), (quantise_plain, 1)]
-            return [(call, pairs[i][which]) for call, which in order]
+        def sort(*units):
+            for unit in units:
+                sort_words(*unit)
 
-        for i in range(len(pairs) + 1):
-            if i < len(pairs):
-                for unit in pairs[i]:
-                    transpose(*unit)
-                if pairs[i][1][1] == PASSES - 1:
-                    spread_bias(pairs[i][1][0])
-            if FIRST_SORTED <= i + 1 < len(pairs):
-                for unit in pairs[i + 1]:
-                    sort_words(*unit)
-            steps = vector_steps(i)
-            if i > 0:
-                b, last = pairs[i - 1][1]
-                now = [last] if i <= PASSES else [last - 1, last]
-            if i < PASSES:
-                for call, unit in steps:
-                    call(*unit)
-                for kind in range(2 if i > 0 else 0):
-                    for t in range(TOKEN_TILES):
-                        multiply(b, t, last, kind)
-            else:
+        def multiply_head(g):
+            for kind in range(2):
                 for t in range(TOKEN_TILES):
-                    if b == W_BLOCKS - 1 and t == TOKEN_TILES - 1:
-                        for cols in (slice(0, PAIR), slice(PAIR, ROWS)) if last == PASSES - 1 else ():
-                            for g in range(PASSES):
-                                for kind in range(2):
-                                    multiply(b, t, g, kind, cols)
-                            finish(b, t, cols)
-                        continue
-                    for g in now:
+                    multiply(0, t, g, kind)
+
+        transpose("x", 0)
+        transpose(0, 0)
+        quantise_signed("x", 0)
+        clear_signs("x", 0)
+        quantise_signed(0, 0)
+        quantise_plain("x", 0)
+        clear_signs(0, 0)
+        quantise_plain(0, 0)
+        prepare(("x", 1), (0, 1), ("x", 2))
+        multiply_head(0)
+        prepare(("x", 3), (0, 2), (0, 3))
+        sort((1, 0), (1, 1))
+        multiply_head(1)
+        spread_bias(0)
+        prepare((1, 0), (1, 1))
+        sort((1, 2), (1, 3))
+        multiply_head(2)
+        for t in range(TOKEN_TILES):
+            multiply(0, t, PASSES - 1, 0)
+            multiply(0, t, PASSES - 1, 1)
+            finish(0, t)
+
+        pairs = [(b, g) for b in range(1, W_BLOCKS) for g in range(0, PASSES, 2)]
+        for i in range(len(pairs)):
+            b, g = pairs[i]
+            if i + 1 < len(pairs):
+                next_b, next_g = pairs[i + 1]
+                prepare((next_b, next_g), (next_b, next_g + 1))
+                if next_g + 2 == PASSES:
+                    spread_bias(next_b)
+            if i + 2 < len(pairs):
+                after_b, after_g = pairs[i + 2]
+                sort((after_b, after_g), (after_b, after_g + 1))
+            ends = g + 2 == PASSES
+            for t in range(TOKEN_TILES):
+                if b == W_BLOCKS - 1 and t == TOKEN_TILES - 1:
+                    for cols in (slice(0, PAIR), slice(PAIR, ROWS)) if ends else ():
+                        for pass_number in range(PASSES):
+                            for kind in range(2):
+                                multiply(b, t, pass_number, kind, cols)
+                        finish(b, t, cols)
+                else:
+                    for pass_number in (g, g + 1):
                         for kind in range(2):
-                            multiply(b, t, g, kind)
-                    for call, unit in steps[2 * t : 2 * t + 2]:
-                        call(*unit)
-                    if last == PASSES - 1:
+                            multiply(b, t, pass_number, kind)
+                    if ends:
                         finish(b, t)

@@ -15,7 +15,7 @@ P = 128
 PACK = 4
 K = 2048
 PASSES = K // (P * PACK)
-HALF = K // 2
+PASS_K = P * PACK
 TOKENS = 512
 OUT = 2048
 ROWS = 512
@@ -23,8 +23,7 @@ ROW_TILES = ROWS // P
 TOKEN_TILES = TOKENS // P
 W_BLOCKS = OUT // ROWS
 PAIR = 256
-ROW_PITCH = HALF + 32
-PASS_WORDS = 256
+ROW_PITCH = 2 * PASS_K + 32
 NO_SIGNS = 0x7FFF7FFF
 
 FLOPS = 2 * 2 * TOKENS * K * OUT
@@ -37,7 +36,8 @@ def tile_skanlinear_kernel(tc, x, weight, out):
 
     with ExitStack() as stack:
         const = stack.enter_context(tc.tile_pool(name="const", bufs=1))
-        raw_pool = stack.enter_context(tc.tile_pool(name="raw", bufs=10))
+        raw_pool = stack.enter_context(tc.tile_pool(name="raw", bufs=7))
+        pass_pool = stack.enter_context(tc.tile_pool(name="pass", bufs=6))
         sorted_pool = stack.enter_context(tc.tile_pool(name="sorted", bufs=6))
         grouped_pool = stack.enter_context(tc.tile_pool(name="grouped", bufs=7))
         plain_pool = stack.enter_context(tc.tile_pool(name="plain", bufs=3))
@@ -55,22 +55,32 @@ def tile_skanlinear_kernel(tc, x, weight, out):
         bias_rows = const.tile([P, OUT], F32)
 
         raws = {}
+        wb_columns = {}
 
-        def load(source, h, first, last, per_dma):
+        def load(source, first, passes, per_dma):
             rows = x2 if source == "x" else weight[source * ROWS : (source + 1) * ROWS, :]
-            view = rows[:, h * HALF + first : h * HALF + last].rearrange("(r p) k -> p r k", p=P)
-            if first == 0:
-                raws[(source, h)] = raw_pool.tile([P, ROW_TILES, ROW_PITCH], BF16, name="raw")
-            raw = raws[(source, h)]
+            start = first * PASS_K
+            end = (first + passes) * PASS_K
+            if first + passes == PASSES:
+                end = rows.shape[1]
+            view = rows[:, start:end].rearrange("(r p) k -> p r k", p=P)
+            if passes == 1:
+                raw = pass_pool.tile([P, ROW_TILES, PASS_K], BF16)
+            else:
+                raw = raw_pool.tile([P, ROW_TILES, ROW_PITCH], BF16)
             for r in range(0, ROW_TILES, per_dma):
-                nc.sync.dma_start(out=raw[:, r : r + per_dma, first:last], in_=view[:, r : r + per_dma, :])
+                nc.sync.dma_start(out=raw[:, r : r + per_dma, 0 : end - start], in_=view[:, r : r + per_dma, :])
+            for g in range(passes):
+                raws[(source, first + g)] = raw[:, :, g * PASS_K : (g + 1) * PASS_K]
+            if end - start > passes * PASS_K:
+                wb_columns[source] = raw[:, :, end - start - 1 : end - start]
 
         def spread_bias(b):
             bank = flip_psum.tile([P, ROWS], F32, tag="bank")
             for r in range(ROW_TILES):
                 nc.tensor.matmul(
                     out=bank[:, r * P : (r + 1) * P],
-                    lhsT=raws[(b, 1)][:, r, HALF : HALF + 1].to_broadcast([P, P]),
+                    lhsT=wb_columns[b][:, r, :].to_broadcast([P, P]),
                     rhs=ident_bf16[:],
                     start=True,
                     stop=True,
@@ -82,8 +92,7 @@ def tile_skanlinear_kernel(tc, x, weight, out):
         ready = {}
 
         def pass_words(source, g):
-            first = (g % 2) * PASS_WORDS * 2
-            return raws[(source, g // 2)][:, :, first : first + PASS_WORDS * 2].bitcast(F32)
+            return raws[(source, g)].bitcast(F32)
 
         def sort_words(source, g):
             done = sorted_pool.tile([P, ROW_TILES, 2, P], F32)
@@ -163,15 +172,16 @@ def tile_skanlinear_kernel(tc, x, weight, out):
 
         stack.enter_context(tc.manual_schedule())
 
-        for g in range(PASSES):
-            first = (g % 2) * (HALF // 2)
-            load("x", g // 2, first, first + HALF // 2, 1)
-            if g < 2:
-                load(0, 0, first, first + HALF // 2, 1)
-        load(0, 1, 0, HALF + 1, 2)
+        load("x", 0, 1, 1)
+        load(0, 0, 1, 2)
+        load("x", 1, 1, 2)
+        load(0, 1, 1, 2)
+        load("x", 2, 1, 2)
+        load("x", 3, 1, 2)
+        load(0, 2, 2, 2)
         for b in range(1, W_BLOCKS):
-            load(b, 0, 0, HALF, ROW_TILES)
-            load(b, 1, 0, HALF + 1, ROW_TILES)
+            load(b, 0, 2, ROW_TILES)
+            load(b, 2, 2, ROW_TILES)
 
         def prepare(*units):
             for unit in units:

@@ -195,10 +195,9 @@ def tile_skanlinear_kernel(tc, x, weight, out):
             for unit in units:
                 sort_words(*unit)
 
-        def multiply_head(g):
-            for kind in range(2):
-                for t in range(TOKEN_TILES):
-                    multiply(0, t, g, kind)
+        def multiply_head(g, kind):
+            for t in range(TOKEN_TILES):
+                multiply(0, t, g, kind)
 
         transpose("x", 0)
         transpose(0, 0)
@@ -208,15 +207,20 @@ def tile_skanlinear_kernel(tc, x, weight, out):
         quantise_plain("x", 0)
         clear_signs(0, 0)
         quantise_plain(0, 0)
-        prepare(("x", 1), (0, 1), ("x", 2))
-        multiply_head(0)
+        prepare(("x", 1), (0, 1))
+        sort(("x", 3))
+        multiply_head(0, 0)
+        prepare(("x", 2))
+        multiply_head(0, 1)
         prepare(("x", 3), (0, 2), (0, 3))
         sort((1, 0), (1, 1))
-        multiply_head(1)
+        multiply_head(1, 0)
+        multiply_head(1, 1)
         spread_bias(0)
         prepare((1, 0), (1, 1))
         sort((1, 2), (1, 3))
-        multiply_head(2)
+        multiply_head(2, 0)
+        multiply_head(2, 1)
         for t in range(TOKEN_TILES):
             multiply(0, t, PASSES - 1, 0)
             multiply(0, t, PASSES - 1, 1)

from contextlib import ExitStack

import concourse.mybir as mybir
from concourse.masks import make_identity

F32 = mybir.dt.float32
BF16 = mybir.dt.bfloat16
I32 = mybir.dt.int32
U8 = mybir.dt.uint8
FP8X4 = mybir.dt.float8_e4m3fn_x4
ALU = mybir.AluOpType
ACT = mybir.ActivationFunctionType

P = 128
PACK = 4
K = 2048
PASSES = K // (P * PACK)
PASS_K = P * PACK
TOKENS = 512
OUT = 2048
ROWS = 512
ROW_TILES = ROWS // P
TOKEN_TILES = TOKENS // P
W_BLOCKS = OUT // ROWS
PAIR = 256
ROW_PITCH = 2 * PASS_K + 32
NO_SIGNS = 0x7FFF7FFF

FLOPS = 2 * 2 * TOKENS * K * OUT


def tile_skanlinear_kernel(tc, x, weight, out):
    nc = tc.nc
    x2 = x.flatten_outer_dims()
    out_tiles = out.rearrange("(t p) o -> p t o", p=P)

    with ExitStack() as stack:
        const = stack.enter_context(tc.tile_pool(name="const", bufs=1))
        raw_pool = stack.enter_context(tc.tile_pool(name="raw", bufs=7))
        pass_pool = stack.enter_context(tc.tile_pool(name="pass", bufs=6))
        sorted_pool = stack.enter_context(tc.tile_pool(name="sorted", bufs=6))
        grouped_pool = stack.enter_context(tc.tile_pool(name="grouped", bufs=7))
        plain_pool = stack.enter_context(tc.tile_pool(name="plain", bufs=3))
        x_pool = stack.enter_context(tc.tile_pool(name="x", bufs=1))
        w_pool = stack.enter_context(tc.tile_pool(name="w", bufs=2))
        y_pool = stack.enter_context(tc.tile_pool(name="y", bufs=4))
        flip_psum = stack.enter_context(tc.psum_pool(name="flip", bufs=4))
        acc_psum = stack.enter_context(tc.psum_pool(name="acc", bufs=4))

        ident_f32 = const.tile([P, P], F32)
        make_identity(nc, ident_f32[:])
        ident_bf16 = const.tile([P, P], BF16)
        make_identity(nc, ident_bf16[:])

        bias_rows = const.tile([P, OUT], F32)

        raws = {}
        wb_columns = {}

        def load(source, first, passes, per_dma):
            rows = x2 if source == "x" else weight[source * ROWS : (source + 1) * ROWS, :]
            start = first * PASS_K
            end = (first + passes) * PASS_K
            if first + passes == PASSES:
                end = rows.shape[1]
            view = rows[:, start:end].rearrange("(r p) k -> p r k", p=P)
            if passes == 1:
                raw = pass_pool.tile([P, ROW_TILES, PASS_K], BF16)
            else:
                raw = raw_pool.tile([P, ROW_TILES, ROW_PITCH], BF16)
            for r in range(0, ROW_TILES, per_dma):
                nc.sync.dma_start(out=raw[:, r : r + per_dma, 0 : end - start], in_=view[:, r : r + per_dma, :])
            for g in range(passes):
                raws[(source, first + g)] = raw[:, :, g * PASS_K : (g + 1) * PASS_K]
            if end - start > passes * PASS_K:
                wb_columns[source] = raw[:, :, end - start - 1 : end - start]

        def spread_bias(b):
            bank = flip_psum.tile([P, ROWS], F32, tag="bank")
            for r in range(ROW_TILES):
                nc.tensor.matmul(
                    out=bank[:, r * P : (r + 1) * P],
                    lhsT=wb_columns[b][:, r, :].to_broadcast([P, P]),
                    rhs=ident_bf16[:],
                    start=True,
                    stop=True,
                )
            nc.scalar.activation(out=bias_rows[:, b * ROWS : (b + 1) * ROWS], in_=bank[:], func=ACT.Relu)

        sorted_words = {}
        grouped_values = {}
        ready = {}

        def pass_words(source, g):
            return raws[(source, g)].bitcast(F32)

        def sort_words(source, g):
            done = sorted_pool.tile([P, ROW_TILES, 2, P], F32)
            nc.scalar.copy(out=done[:], in_=pass_words(source, g).rearrange("p r (w u) -> p r u w", u=2))
            sorted_words[(source, g)] = done

        def transpose(source, g):
            grouped = grouped_pool.tile([P, ROWS, PACK], BF16, align_bytes=64)
            words = grouped[:].rearrange("p o t -> p (o t)").bitcast(F32).rearrange("p (o u) -> p o u", u=2)
            for first in range(0, ROWS, PAIR):
                bank = flip_psum.tile([P, 2, PAIR], F32, tag="bank")
                for u in range(2):
                    for r in range(PAIR // P):
                        tile_number = first // P + r
                        if (source, g) in sorted_words:
                            part = sorted_words[(source, g)][:, tile_number, u, :]
                        else:
                            part = pass_words(source, g)[:, tile_number, u::2]
                        nc.tensor.transpose(bank[:, u, r * P : (r + 1) * P], part, ident_f32[:])
                nc.scalar.copy(out=words[:, first : first + PAIR, :], in_=bank[:].rearrange("p u o -> p o u"))
            grouped_values[(source, g)] = grouped

        def quantise_one(pool, name, values):
            codes = pool.tile([P, ROWS], I32, name="codes_" + name, align_bytes=64)
            scales = pool.tile([P, ROWS], U8, name="scales_" + name, align_bytes=64)
            nc.vector.quantize_mx(
                out=codes[:].bitcast(FP8X4), scales=scales[:], in_=values[:].rearrange("p o t -> p (o t)")
            )
            return (codes, scales)

        plain_values = {}

        def quantise_signed(source, g):
            pool, name = (x_pool, "x%d" % g) if source == "x" else (w_pool, "w%d" % g)
            ready[(source, g, 0)] = quantise_one(pool, name, grouped_values[(source, g)])

        def clear_signs(source, g):
            plain = plain_pool.tile([P, ROWS, PACK], BF16, align_bytes=64)
            nc.vector.tensor_scalar(
                out=plain[:].bitcast(I32),
                in0=grouped_values[(source, g)][:].bitcast(I32),
                scalar1=NO_SIGNS,
                scalar2=None,
                op0=ALU.bitwise_and,
            )
            plain_values[(source, g)] = plain

        def quantise_plain(source, g):
            pool, name = (x_pool, "abs_x%d" % g) if source == "x" else (w_pool, "abs_w%d" % g)
            ready[(source, g, 1)] = quantise_one(pool, name, plain_values[(source, g)])

        acc = {}

        def multiply(b, t, g, kind, cols=slice(0, ROWS)):
            tokens = slice(t * P, (t + 1) * P)
            if g == 0 and kind == 0:
                acc[t] = acc_psum.tile([P, cols.stop - cols.start], F32, name="acc")
            x_codes, x_scales = ready[("x", g, kind)]
            w_codes, w_scales = ready[(b, g, kind)]
            nc.tensor.matmul_mx(
                out=acc[t][:],
                lhsT=x_codes[:, tokens].bitcast(FP8X4),
                lhsT_scale=x_scales[:, tokens],
                rhs=w_codes[:, cols].bitcast(FP8X4),
                rhs_scale=w_scales[:, cols],
                start=(g == 0 and kind == 0),
                stop=(g == PASSES - 1 and kind == 1),
            )

        def finish(b, t, cols=slice(0, ROWS)):
            out_cols = slice(b * ROWS + cols.start, b * ROWS + cols.stop)
            y = y_pool.tile([P, cols.stop - cols.start], F32)
            nc.vector.scalar_tensor_tensor(
                out=y[:], in0=acc[t][:], scalar=0.5, in1=bias_rows[:, out_cols], op0=ALU.mult, op1=ALU.add
            )
            nc.sync.dma_start(out=out_tiles[:, t, out_cols], in_=y[:])

        stack.enter_context(tc.manual_schedule())

        load("x", 0, 1, 1)
        load(0, 0, 1, 2)
        load("x", 1, 1, 2)
        load(0, 1, 1, 2)
        load("x", 2, 1, 2)
        load("x", 3, 1, 2)
        load(0, 2, 2, 2)
        for b in range(1, W_BLOCKS):
            load(b, 0, 2, ROW_TILES)
            load(b, 2, 2, ROW_TILES)

        def prepare(*units):
            for unit in units:
                transpose(*unit)
            for unit in units:
                clear_signs(*unit)
                quantise_signed(*unit)
                quantise_plain(*unit)

        def sort(*units):
            for unit in units:
                sort_words(*unit)

        def multiply_head(g, kind):
            for t in range(TOKEN_TILES):
                multiply(0, t, g, kind)

        transpose("x", 0)
        transpose(0, 0)
        quantise_signed("x", 0)
        clear_signs("x", 0)
        quantise_signed(0, 0)
        quantise_plain("x", 0)
        clear_signs(0, 0)
        quantise_plain(0, 0)
        prepare(("x", 1), (0, 1))
        sort(("x", 3))
        multiply_head(0, 0)
        prepare(("x", 2))
        multiply_head(0, 1)
        prepare(("x", 3), (0, 2), (0, 3))
        sort((1, 0), (1, 1))
        multiply_head(1, 0)
        multiply_head(1, 1)
        spread_bias(0)
        prepare((1, 0), (1, 1))
        sort((1, 2), (1, 3))
        multiply_head(2, 0)
        multiply_head(2, 1)
        for t in range(TOKEN_TILES):
            multiply(0, t, PASSES - 1, 0)
            multiply(0, t, PASSES - 1, 1)
            finish(0, t)

        pairs = [(b, g) for b in range(1, W_BLOCKS) for g in range(0, PASSES, 2)]
        for i in range(len(pairs)):
            b, g = pairs[i]
            if i + 1 < len(pairs):
                next_b, next_g = pairs[i + 1]
                prepare((next_b, next_g), (next_b, next_g + 1))
                if next_g + 2 == PASSES:
                    spread_bias(next_b)
            if i + 2 < len(pairs):
                after_b, after_g = pairs[i + 2]
                sort((after_b, after_g), (after_b, after_g + 1))
            ends = g + 2 == PASSES
            for t in range(TOKEN_TILES):
                if b == W_BLOCKS - 1 and t == TOKEN_TILES - 1:
                    for cols in (slice(0, PAIR), slice(PAIR, ROWS)) if ends else ():
                        for pass_number in range(PASSES):
                            for kind in range(2):
                                multiply(b, t, pass_number, kind, cols)
                        finish(b, t, cols)
                else:
                    for pass_number in (g, g + 1):
                        for kind in range(2):
                            multiply(b, t, pass_number, kind)
                    if ends:
                        finish(b, t)
